import numpy as np
import ml_dtypes


def mxq(x, axis, fmt="e4m3"):
    dtype, down = {"e4m3": (ml_dtypes.float8_e4m3fn, 7), "e5m2": (ml_dtypes.float8_e5m2, 14)}[fmt]
    v = np.moveaxis(np.asarray(x, np.float32).astype(ml_dtypes.bfloat16).astype(np.float64), axis, -1)
    blocks = v.reshape(v.shape[:-1] + (-1, 32))
    amax = np.abs(blocks).max(-1, keepdims=True)
    byte = np.maximum(np.where(amax > 0, np.frexp(amax)[1] - 1 + 127, 0) - down, 1)
    scale = np.exp2(byte - 127.0)
    codes = (blocks / scale).astype(np.float32).astype(dtype).astype(np.float64)
    return np.moveaxis((codes * scale).reshape(v.shape), -1, axis)


WIDE = False


def mx_kscale(k):
    if not WIDE:
        return np.ones(k)
    levels = np.array([10, -10, 5, -5, 0])
    if k % 512:
        return np.exp2(np.random.permutation(np.resize(levels, k // 32))).repeat(32)
    a = np.empty((k // 512, 16))
    for p in range(k // 512):
        a[p, :8] = np.random.permutation(np.resize(levels, 8))
        for g in range(8):
            far = levels[np.abs(levels - a[p, g]) >= 10]
            a[p, g + 8] = far[np.random.randint(len(far))]
    return np.exp2(a.ravel()).repeat(32)


BF16 = ml_dtypes.bfloat16


def bf(x):
    return np.asarray(x, np.float32).astype(BF16)


def f64(x):
    return np.asarray(x).astype(np.float64)


B, S, E, HID, H = 2, 512, 2048, 2048, 16
DH = HID // H


def setup_inputs():
    t = mx_kscale(HID)
    kv_rms = np.hypot(6.0 * np.sqrt(S), 0.19 * S)
    return {"q_feat": bf(1.0 + 2.8 * np.random.standard_normal((B, H, S, DH))),
            "kv": bf(np.random.standard_normal((B, H, DH, DH)) * kv_rms * t.reshape(H, 1, DH)),
            "denom": bf(S * DH * (1.0 + 0.1 * np.random.standard_normal((B, H, 1, 1)))),
            "Wo": bf(np.random.standard_normal((HID, E)) * 4.0 / np.sqrt(HID) / t[:, None]),
            "bo": bf(np.random.standard_normal(E) * 0.1)}


def reference(q_feat, kv, denom, Wo, bo):
    qkv = f64(q_feat) @ f64(kv)
    ctx = qkv / f64(denom)
    ctx = ctx.transpose(0, 2, 1, 3).reshape(B, S, HID)
    return (mxq(ctx, 2, "e4m3") @ mxq(f64(Wo), 0, "e4m3")) + f64(bo)

@@ -1,0 +1,297 @@
+from contextlib import ExitStack
+
+import concourse.mybir as mybir
+from concourse.masks import make_identity
+
+BF16 = mybir.dt.bfloat16
+F32 = mybir.dt.float32
+U32 = mybir.dt.uint32
+U8 = mybir.dt.uint8
+FP8X4 = mybir.dt.float8_e4m3fn_x4
+COPY = mybir.ActivationFunctionType.Copy
+
+B, H, S, DH = 2, 16, 512, 128
+HID = H * DH
+E = 2048
+
+P = 128
+PACK = 4
+PASSES = HID // (P * PACK)
+ROW_TILES = S // P
+N_TILE = 512
+N_CHUNKS = E // N_TILE
+GROUPS = B * PASSES
+HEADS = B * H
+WO_LOAD = 1024
+AHEAD = 3
+
+FLOPS = 2 * B * H * S * DH * DH + 2 * B * S * HID * E
+
+
+def tile_linearattention_pb_kernel(tc, q_feat, kv, denom, Wo, bo, out):
+    nc = tc.nc
+    with ExitStack() as stack:
+        stack.enter_context(tc.manual_schedule())
+        keep = stack.enter_context(tc.tile_pool(name="keep", bufs=1))
+        early_pool = stack.enter_context(tc.tile_pool(name="early", bufs=GROUPS // 2))
+        qt_pool = stack.enter_context(tc.tile_pool(name="qt", bufs=AHEAD + 2))
+        c_pool = stack.enter_context(tc.tile_pool(name="c", bufs=3))
+        grouped_pool = stack.enter_context(tc.tile_pool(name="grouped", bufs=6))
+        res_pool = stack.enter_context(tc.tile_pool(name="res", bufs=8))
+        psum_a = stack.enter_context(tc.psum_pool(name="psum_a", bufs=4))
+        psum_b = stack.enter_context(tc.psum_pool(name="psum_b", bufs=4))
+
+        den_bf = keep.tile([P, HEADS], BF16, name="den_bf")
+        nc.scalar.dma_start(
+            out=den_bf[:], in_=denom.rearrange("b h x y -> (b h x y)").partition_broadcast(P)
+        )
+        bias_row = keep.tile([P, E], BF16, name="bias_row")
+
+        kv_sb = [keep.tile([P, H, DH], BF16, name="kv_sb%d" % b) for b in range(B)]
+        q_sb = []
+
+        def load_q(u, t0, count):
+            b, g = divmod(u, PASSES)
+            heads = slice(PACK * g + t0, PACK * g + t0 + count)
+            slot = PACK * (g % 2) + t0
+            nc.sync.dma_start(
+                out=q_sb[u // 2][:, slot : slot + count, :],
+                in_=q_feat[b, heads].rearrange("t (p i) d -> p t (i d)", i=ROW_TILES),
+            )
+
+        def load_kv(u):
+            b, g = divmod(u, PASSES)
+            heads = slice(PACK * g, PACK * (g + 1))
+            nc.sync.dma_start(out=kv_sb[b][:, heads, :], in_=kv[b, heads].rearrange("t d e -> d t e"))
+
+        wo_rows = Wo.rearrange("(g p t) n -> g p t n", p=P, t=PACK)
+        wo_raw = {}
+
+        def load_wo(half, g):
+            if half == 0:
+                raw = keep.tile([P, PACK, WO_LOAD], BF16, name="wo_raw%d" % g)
+            else:
+                raw = early_pool.tile([P, PACK, WO_LOAD], BF16, name="wo_raw", tag="early")
+            nc.sync.dma_start(out=raw[:], in_=wo_rows[g, :, :, half * WO_LOAD : (half + 1) * WO_LOAD])
+            wo_raw[half, g] = raw
+
+        for u in range(GROUPS):
+            if u % 2 == 0:
+                q_pair = early_pool.tile([P, 2 * PACK, S], BF16, name="q_pair", tag="early")
+                q_sb.append(q_pair)
+            if u == 0:
+                load_q(u, 0, 1)
+                load_q(u, 1, 1)
+                load_kv(u)
+                load_q(u, 2, 1)
+                load_q(u, 3, 1)
+            else:
+                load_q(u, 0, PACK)
+                load_kv(u)
+            if u == 3:
+                load_wo(0, 0)
+            if u == 5:
+                load_wo(0, 1)
+        load_wo(0, 2)
+        load_wo(0, 3)
+        ones = keep.tile([P, P], BF16, name="ones")
+        nc.vector.memset(ones[:], 1.0)
+        bias_sb = keep.tile([P, E], F32, name="bias_sb")
+        ident = keep.tile([P, P], BF16, name="ident")
+        make_identity(nc, ident[:])
+        ident_w = keep.tile([P, P], F32, name="ident_w")
+        make_identity(nc, ident_w[:])
+        nc.gpsimd.memset(bias_row[:], 0.0)
+        nc.gpsimd.dma_start(out=bias_row[0:1, :], in_=bo.rearrange("(o n) -> o n", o=1))
+        rden = keep.tile([P, HEADS], F32, name="rden")
+        nc.vector.reciprocal(out=rden[:], in_=den_bf[:])
+
+        ctx_codes = keep.tile([P, GROUPS, S], U32, name="ctx_codes", align_bytes=64)
+        ctx_scales = keep.tile([P, GROUPS, S], U8, name="ctx_scales", align_bytes=64)
+        wo_codes = keep.tile([P, N_CHUNKS * PASSES, N_TILE], U32, name="wo_codes", align_bytes=64)
+        wo_scales = keep.tile([P, N_CHUNKS * PASSES, N_TILE], U8, name="wo_scales", align_bytes=64)
+
+        qT_tiles = []
+        c_tiles = []
+        ctx_grouped = []
+        wo_grouped = {}
+
+        def transpose_head(n):
+            u, t = divmod(n, PACK)
+            slot = PACK * (u % 2) + t
+            qT_ps = psum_a.tile([P, ROW_TILES, P], BF16, name="qT_ps", tag="a")
+            for i in range(ROW_TILES):
+                nc.tensor.transpose(
+                    qT_ps[:, i, :], q_sb[u // 2][:, slot, i * DH : (i + 1) * DH], ident[:]
+                )
+            qT = qt_pool.tile([P, ROW_TILES, P], BF16, name="qT")
+            nc.scalar.copy(out=qT[:], in_=qT_ps[:])
+            qT_tiles.append(qT)
+
+        def multiply_head(n):
+            u, t = divmod(n, PACK)
+            b, g = divmod(u, PASSES)
+            h = PACK * g + t
+            if t == 0:
+                c_tiles.append(c_pool.tile([P, ROW_TILES, 2, P * 2], BF16, name="c", align_bytes=64))
+            ps = psum_b.tile([P, ROW_TILES, 2, DH // 2], F32, name="ps", tag="b")
+            for i in range(ROW_TILES):
+                nc.tensor.matmul(
+                    ps[:, i, :, :].rearrange("s u (p e) -> s p u e", e=2),
+                    lhsT=qT_tiles[n][:, i, :],
+                    rhs=kv_sb[b][:, h, :].rearrange("d (p u e) -> d p u e", u=2, e=2),
+                    start=True,
+                    stop=True,
+                )
+            dst = c_tiles[u][:, :, :, t * (DH // 2) : (t + 1) * (DH // 2)]
+            scale = rden[:, n : n + 1]
+            if t == 1:
+                nc.vector.tensor_scalar(
+                    out=dst, in0=ps[:], scalar1=scale, scalar2=None, op0=mybir.AluOpType.mult
+                )
+            else:
+                nc.scalar.activation(out=dst, in_=ps[:], func=COPY, scale=scale)
+
+        def turn_back(u, half):
+            if half == 0:
+                ctx_grouped.append(
+                    grouped_pool.tile([P, S, PACK], BF16, name="grouped", tag="grouped", align_bytes=64)
+                )
+            words = c_tiles[u][:].rearrange("s i u k -> s (i u k)").bitcast(F32)
+            back = psum_a.tile([P, 2, 2, P], F32, name="back", tag="a")
+            for ii in range(2):
+                for w in range(2):
+                    first = ((2 * half + ii) * 2 + w) * P
+                    nc.tensor.transpose(back[:, ii, w, :], words[:, first : first + P], ident_w[:])
+            dst = ctx_grouped[u][:].rearrange("p s t -> p (s t)").bitcast(F32)
+            width = S * 2 // 2
+            nc.vector.tensor_copy(
+                out=dst[:, half * width : (half + 1) * width].rearrange("p (i s w) -> p i s w", i=2, w=2),
+                in_=back[:].rearrange("p i w s -> p i s w"),
+            )
+
+        def quantise_ctx(u):
+            nc.vector.quantize_mx(
+                out=ctx_codes[:, u, :].bitcast(FP8X4),
+                scales=ctx_scales[:, u, :],
+                in_=ctx_grouped[u][:].rearrange("p s t -> p (s t)"),
+            )
+
+        def broadcast_bias(j):
+            cols = slice(j * N_TILE, (j + 1) * N_TILE)
+            bias_ps = psum_a.tile([P, N_TILE], F32, name="bias_ps", tag="a")
+            nc.tensor.matmul(bias_ps[:], lhsT=ones[:], rhs=bias_row[:, cols], start=True, stop=True)
+            nc.vector.tensor_copy(out=bias_sb[:, cols], in_=bias_ps[:])
+
+        def regroup(copy, w, c0, c1):
+            j, g = divmod(w, PASSES)
+            if c0 == 0:
+                wo_grouped[w] = grouped_pool.tile(
+                    [P, N_TILE, PACK], BF16, name="grouped", tag="grouped", align_bytes=64
+                )
+            half, col = divmod(j * N_TILE, WO_LOAD)
+            copy(
+                out=wo_grouped[w][:, c0:c1, :].rearrange("p (c r) t -> p c t r", r=4),
+                in_=wo_raw[half, g][:, :, col + c0 : col + c1].rearrange("p t (c r) -> p c t r", r=4),
+            )
+
+        def quantise_wo(w):
+            nc.vector.quantize_mx(
+                out=wo_codes[:, w, :].bitcast(FP8X4),
+                scales=wo_scales[:, w, :],
+                in_=wo_grouped[w][:].rearrange("p n t -> p (n t)"),
+            )
+
+        def new_sums(b):
+            pool, tag = (psum_b, "b") if b == 0 else (psum_a, "a")
+            return [pool.tile([P, N_TILE], F32, name="sums", tag=tag) for i in range(ROW_TILES)]
+
+        def one_pass(b, j, sums, g, i):
+            u = b * PASSES + g
+            w = j * PASSES + g
+            rows = slice(i * P, (i + 1) * P)
+            nc.tensor.matmul_mx(
+                out=sums[i][:],
+                lhsT=ctx_codes[:, u, rows].bitcast(FP8X4),
+                lhsT_scale=ctx_scales[:, u, rows],
+                rhs=wo_codes[:, w, :].bitcast(FP8X4),
+                rhs_scale=wo_scales[:, w, :],
+                start=(g == 0),
+                stop=(g == PASSES - 1),
+            )
+
+        def add_bias_and_store(b, j, sums, i0):
+            cols = slice(j * N_TILE, (j + 1) * N_TILE)
+            res = res_pool.tile([P, 2, N_TILE], F32, name="res", align_bytes=64)
+            for i in (i0, i0 + 1):
+                nc.vector.tensor_tensor(
+                    out=res[:, i - i0, :], in0=sums[i][:], in1=bias_sb[:, cols],
+                    op=mybir.AluOpType.add,
+                )
+            out_rows = out[b].rearrange("(p i) n -> p i n", i=ROW_TILES)
+            nc.sync.dma_start(out=out_rows[:, i0 : i0 + 2, cols], in_=res[:])
+
+        for n in range(AHEAD):
+            transpose_head(n)
+        for n in range(HEADS):
+            if n + AHEAD < HEADS:
+                transpose_head(n + AHEAD)
+            multiply_head(n)
+            u, t = divmod(n, PACK)
+            if u >= 1 and t in (1, 2):
+                turn_back(u - 1, t - 1)
+            if t == 3:
+                if u >= 1:
+                    quantise_ctx(u - 1)
+                if u < N_CHUNKS:
+                    broadcast_bias(u)
+                else:
+                    w, part = divmod(u - N_CHUNKS, 2)
+                    regroup(nc.vector.tensor_copy, w, part * N_TILE // 2, (part + 1) * N_TILE // 2)
+        for g in range(PASSES):
+            load_wo(1, g)
+        regroup(nc.scalar.copy, 2, 0, N_TILE)
+        regroup(nc.scalar.copy, 3, 0, N_TILE)
+        quantise_wo(0)
+        sums = new_sums(0)
+        for i in range(ROW_TILES):
+            one_pass(0, 0, sums, 0, i)
+        turn_back(GROUPS - 1, 0)
+        turn_back(GROUPS - 1, 1)
+        quantise_wo(1)
+        quantise_wo(2)
+        quantise_ctx(GROUPS - 1)
+        quantise_wo(3)
+
+        for j in range(N_CHUNKS):
+            for b in range(B):
+                if (j, b) == (0, 0):
+                    order = [(g, i) for g in range(1, PASSES) for i in range(ROW_TILES)]
+                elif (j, b) != (N_CHUNKS - 1, B - 1):
+                    sums = new_sums(b)
+                    order = [(g, i) for g in range(PASSES) for i in range(ROW_TILES)]
+                else:
+                    sums = new_sums(b)
+                    order = [(g, i) for i in range(ROW_TILES) for g in range(PASSES)]
+                for g, i in order:
+                    one_pass(b, j, sums, g, i)
+                first = (j + 1) * PASSES
+                more = j + 1 < N_CHUNKS
+                if more and b == 0:
+                    regroup(nc.scalar.copy, first + 1, 0, N_TILE)
+                    regroup(nc.vector.tensor_copy, first, 0, N_TILE // 2)
+                    regroup(nc.vector.tensor_copy, first, N_TILE // 2, N_TILE)
+                    add_bias_and_store(b, j, sums, 0)
+                    quantise_wo(first)
+                    add_bias_and_store(b, j, sums, 2)
+                elif more:
+                    regroup(nc.scalar.copy, first + 2, 0, N_TILE)
+                    regroup(nc.scalar.copy, first + 3, 0, N_TILE)
+                    quantise_wo(first + 1)
+                    add_bias_and_store(b, j, sums, 0)
+                    quantise_wo(first + 2)
+                    add_bias_and_store(b, j, sums, 2)
+                    quantise_wo(first + 3)
+                else:
+                    add_bias_and_store(b, j, sums, 0)
+                    add_bias_and_store(b, j, sums, 2)

@@ -23,7 +23,9 @@ N_CHUNKS = E // N_TILE
 GROUPS = B * PASSES
 HEADS = B * H
 WO_LOAD = 1024
-AHEAD = 3
+PAIRS = HEADS // 2
+AHEAD = 2
+PIECES = 4
 
 FLOPS = 2 * B * H * S * DH * DH + 2 * B * S * HID * E
 
@@ -36,16 +38,20 @@ def tile_linearattention_pb_kernel(tc, q_feat, kv, denom, Wo, bo, out):
         early_pool = stack.enter_context(tc.tile_pool(name="early", bufs=GROUPS // 2))
         qt_pool = stack.enter_context(tc.tile_pool(name="qt", bufs=AHEAD + 2))
         c_pool = stack.enter_context(tc.tile_pool(name="c", bufs=3))
-        grouped_pool = stack.enter_context(tc.tile_pool(name="grouped", bufs=6))
+        grouped_pool = stack.enter_context(tc.tile_pool(name="grouped", bufs=7))
         res_pool = stack.enter_context(tc.tile_pool(name="res", bufs=8))
-        psum_a = stack.enter_context(tc.psum_pool(name="psum_a", bufs=4))
-        psum_b = stack.enter_context(tc.psum_pool(name="psum_b", bufs=4))
+        psum_t = stack.enter_context(tc.psum_pool(name="psum_t", bufs=2))
+        psum_r = stack.enter_context(tc.psum_pool(name="psum_r", bufs=2))
+        psum_m = stack.enter_context(tc.psum_pool(name="psum_m", bufs=4))
 
         den_bf = keep.tile([P, HEADS], BF16, name="den_bf")
         nc.scalar.dma_start(
             out=den_bf[:], in_=denom.rearrange("b h x y -> (b h x y)").partition_broadcast(P)
         )
-        bias_row = keep.tile([P, E], BF16, name="bias_row")
+        dummy = keep.tile([P, 2], F32, name="dummy")
+        nc.vector.memset(dummy[:], 1.0)
+        nc.scalar.copy(out=dummy[:, 1:2], in_=dummy[:, 0:1])
+        bias_sb = keep.tile([P, E], BF16, name="bias_sb")
 
         kv_sb = [keep.tile([P, H, DH], BF16, name="kv_sb%d" % b) for b in range(B)]
         q_sb = []
@@ -80,29 +86,21 @@ def tile_linearattention_pb_kernel(tc, q_feat, kv, denom, Wo, bo, out):
                 q_pair = early_pool.tile([P, 2 * PACK, S], BF16, name="q_pair", tag="early")
                 q_sb.append(q_pair)
             if u == 0:
-                load_q(u, 0, 1)
-                load_q(u, 1, 1)
+                load_q(u, 0, 2)
                 load_kv(u)
-                load_q(u, 2, 1)
-                load_q(u, 3, 1)
+                load_q(u, 2, 2)
             else:
                 load_q(u, 0, PACK)
                 load_kv(u)
-            if u == 3:
-                load_wo(0, 0)
-            if u == 5:
-                load_wo(0, 1)
-        load_wo(0, 2)
+            if u in (3, 4, 5):
+                load_wo(0, u - 3)
+            if u == 4:
+                nc.sync.dma_start(out=bias_sb[:], in_=bo.partition_broadcast(P))
         load_wo(0, 3)
-        ones = keep.tile([P, P], BF16, name="ones")
-        nc.vector.memset(ones[:], 1.0)
-        bias_sb = keep.tile([P, E], F32, name="bias_sb")
         ident = keep.tile([P, P], BF16, name="ident")
         make_identity(nc, ident[:])
         ident_w = keep.tile([P, P], F32, name="ident_w")
         make_identity(nc, ident_w[:])
-        nc.gpsimd.memset(bias_row[:], 0.0)
-        nc.gpsimd.dma_start(out=bias_row[0:1, :], in_=bo.rearrange("(o n) -> o n", o=1))
         rden = keep.tile([P, HEADS], F32, name="rden")
         nc.vector.reciprocal(out=rden[:], in_=den_bf[:])
 
@@ -116,15 +114,16 @@ def tile_linearattention_pb_kernel(tc, q_feat, kv, denom, Wo, bo, out):
         ctx_grouped = []
         wo_grouped = {}
 
-        def transpose_head(n):
-            u, t = divmod(n, PACK)
+        def transpose_pair(m):
+            u, t = divmod(2 * m, PACK)
             slot = PACK * (u % 2) + t
-            qT_ps = psum_a.tile([P, ROW_TILES, P], BF16, name="qT_ps", tag="a")
-            for i in range(ROW_TILES):
-                nc.tensor.transpose(
-                    qT_ps[:, i, :], q_sb[u // 2][:, slot, i * DH : (i + 1) * DH], ident[:]
-                )
-            qT = qt_pool.tile([P, ROW_TILES, P], BF16, name="qT")
+            qT_ps = psum_t.tile([P, 2, ROW_TILES, P], BF16, name="qT_ps", tag="t")
+            for tt in range(2):
+                for i in range(ROW_TILES):
+                    nc.tensor.transpose(
+                        qT_ps[:, tt, i, :], q_sb[u // 2][:, slot + tt, i * DH : (i + 1) * DH], ident[:]
+                    )
+            qT = qt_pool.tile([P, 2, ROW_TILES, P], BF16, name="qT")
             nc.scalar.copy(out=qT[:], in_=qT_ps[:])
             qT_tiles.append(qT)
 
@@ -134,18 +133,18 @@ def tile_linearattention_pb_kernel(tc, q_feat, kv, denom, Wo, bo, out):
             h = PACK * g + t
             if t == 0:
                 c_tiles.append(c_pool.tile([P, ROW_TILES, 2, P * 2], BF16, name="c", align_bytes=64))
-            ps = psum_b.tile([P, ROW_TILES, 2, DH // 2], F32, name="ps", tag="b")
+            ps = psum_m.tile([P, ROW_TILES, 2, DH // 2], F32, name="ps", tag="m")
             for i in range(ROW_TILES):
                 nc.tensor.matmul(
                     ps[:, i, :, :].rearrange("s u (p e) -> s p u e", e=2),
-                    lhsT=qT_tiles[n][:, i, :],
+                    lhsT=qT_tiles[n // 2][:, n % 2, i, :],
                     rhs=kv_sb[b][:, h, :].rearrange("d (p u e) -> d p u e", u=2, e=2),
                     start=True,
                     stop=True,
                 )
             dst = c_tiles[u][:, :, :, t * (DH // 2) : (t + 1) * (DH // 2)]
             scale = rden[:, n : n + 1]
-            if t == 1:
+            if t % 2 == 0:
                 nc.vector.tensor_scalar(
                     out=dst, in0=ps[:], scalar1=scale, scalar2=None, op0=mybir.AluOpType.mult
                 )
@@ -158,14 +157,15 @@ def tile_linearattention_pb_kernel(tc, q_feat, kv, denom, Wo, bo, out):
                     grouped_pool.tile([P, S, PACK], BF16, name="grouped", tag="grouped", align_bytes=64)
                 )
             words = c_tiles[u][:].rearrange("s i u k -> s (i u k)").bitcast(F32)
-            back = psum_a.tile([P, 2, 2, P], F32, name="back", tag="a")
+            back = psum_r.tile([P, 2, 2, P], F32, name="back", tag="r")
             for ii in range(2):
                 for w in range(2):
                     first = ((2 * half + ii) * 2 + w) * P
                     nc.tensor.transpose(back[:, ii, w, :], words[:, first : first + P], ident_w[:])
             dst = ctx_grouped[u][:].rearrange("p s t -> p (s t)").bitcast(F32)
             width = S * 2 // 2
-            nc.vector.tensor_copy(
+            copy = nc.vector.tensor_copy if half == 0 else nc.scalar.copy
+            copy(
                 out=dst[:, half * width : (half + 1) * width].rearrange("p (i s w) -> p i s w", i=2, w=2),
                 in_=back[:].rearrange("p i w s -> p i s w"),
             )
@@ -177,23 +177,22 @@ def tile_linearattention_pb_kernel(tc, q_feat, kv, denom, Wo, bo, out):
                 in_=ctx_grouped[u][:].rearrange("p s t -> p (s t)"),
             )
 
-        def broadcast_bias(j):
-            cols = slice(j * N_TILE, (j + 1) * N_TILE)
-            bias_ps = psum_a.tile([P, N_TILE], F32, name="bias_ps", tag="a")
-            nc.tensor.matmul(bias_ps[:], lhsT=ones[:], rhs=bias_row[:, cols], start=True, stop=True)
-            nc.vector.tensor_copy(out=bias_sb[:, cols], in_=bias_ps[:])
-
-        def regroup(copy, w, c0, c1):
+        def regroup(copy, w, c0, c1, on_gpsimd=False):
             j, g = divmod(w, PASSES)
             if c0 == 0:
                 wo_grouped[w] = grouped_pool.tile(
                     [P, N_TILE, PACK], BF16, name="grouped", tag="grouped", align_bytes=64
                 )
             half, col = divmod(j * N_TILE, WO_LOAD)
-            copy(
-                out=wo_grouped[w][:, c0:c1, :].rearrange("p (c r) t -> p c t r", r=4),
-                in_=wo_raw[half, g][:, :, col + c0 : col + c1].rearrange("p t (c r) -> p c t r", r=4),
-            )
+            extra = {}
+            if on_gpsimd:
+                extra = {"scalar1": 1.0, "scalar2": 0.0, "op0": mybir.AluOpType.mult, "op1": mybir.AluOpType.add}
+            dst = wo_grouped[w][:, c0:c1, :].rearrange("p (c r) t -> p c t r", r=4)
+            src = wo_raw[half, g][:, :, col + c0 : col + c1].rearrange("p t (c r) -> p c t r", r=4)
+            if on_gpsimd:
+                copy(dst, src, **extra)
+            else:
+                copy(out=dst, in_=src)
 
         def quantise_wo(w):
             nc.vector.quantize_mx(
@@ -203,8 +202,11 @@ def tile_linearattention_pb_kernel(tc, q_feat, kv, denom, Wo, bo, out):
             )
 
         def new_sums(b):
-            pool, tag = (psum_b, "b") if b == 0 else (psum_a, "a")
-            return [pool.tile([P, N_TILE], F32, name="sums", tag=tag) for i in range(ROW_TILES)]
+            if b == 0:
+                homes = [(psum_m, "m")] * ROW_TILES
+            else:
+                homes = [(psum_t, "t"), (psum_r, "r")] * 2
+            return [pool.tile([P, N_TILE], F32, name="sums", tag=tag) for pool, tag in homes]
 
         def one_pass(b, j, sums, g, i):
             u = b * PASSES + g
@@ -231,37 +233,35 @@ def tile_linearattention_pb_kernel(tc, q_feat, kv, denom, Wo, bo, out):
             out_rows = out[b].rearrange("(p i) n -> p i n", i=ROW_TILES)
             nc.sync.dma_start(out=out_rows[:, i0 : i0 + 2, cols], in_=res[:])
 
-        for n in range(AHEAD):
-            transpose_head(n)
-        for n in range(HEADS):
-            if n + AHEAD < HEADS:
-                transpose_head(n + AHEAD)
-            multiply_head(n)
-            u, t = divmod(n, PACK)
-            if u >= 1 and t in (1, 2):
-                turn_back(u - 1, t - 1)
-            if t == 3:
-                if u >= 1:
-                    quantise_ctx(u - 1)
-                if u < N_CHUNKS:
-                    broadcast_bias(u)
-                else:
-                    w, part = divmod(u - N_CHUNKS, 2)
-                    regroup(nc.vector.tensor_copy, w, part * N_TILE // 2, (part + 1) * N_TILE // 2)
+        for w in range(PASSES):
+            for piece in range(PIECES):
+                regroup(
+                    nc.gpsimd.tensor_scalar, w, piece * N_TILE // PIECES, (piece + 1) * N_TILE // PIECES, True
+                )
+        for m in range(AHEAD):
+            transpose_pair(m)
+        for m in range(PAIRS):
+            if m + AHEAD < PAIRS:
+                transpose_pair(m + AHEAD)
+            multiply_head(2 * m)
+            multiply_head(2 * m + 1)
+            u, second = divmod(m, 2)
+            if u >= 1:
+                turn_back(u - 1, second)
+            if u >= 2 and second == 0:
+                quantise_ctx(u - 2)
+            if u in (5, 6, 7) and second == 1:
+                quantise_wo(u - 5)
         for g in range(PASSES):
             load_wo(1, g)
-        regroup(nc.scalar.copy, 2, 0, N_TILE)
-        regroup(nc.scalar.copy, 3, 0, N_TILE)
-        quantise_wo(0)
         sums = new_sums(0)
         for i in range(ROW_TILES):
             one_pass(0, 0, sums, 0, i)
         turn_back(GROUPS - 1, 0)
         turn_back(GROUPS - 1, 1)
-        quantise_wo(1)
-        quantise_wo(2)
-        quantise_ctx(GROUPS - 1)
+        quantise_ctx(GROUPS - 2)
         quantise_wo(3)
+        quantise_ctx(GROUPS - 1)
 
         for j in range(N_CHUNKS):
             for b in range(B):
@@ -278,9 +278,8 @@ def tile_linearattention_pb_kernel(tc, q_feat, kv, denom, Wo, bo, out):
                 first = (j + 1) * PASSES
                 more = j + 1 < N_CHUNKS
                 if more and b == 0:
+                    regroup(nc.scalar.copy, first, 0, N_TILE)
                     regroup(nc.scalar.copy, first + 1, 0, N_TILE)
-                    regroup(nc.vector.tensor_copy, first, 0, N_TILE // 2)
-                    regroup(nc.vector.tensor_copy, first, N_TILE // 2, N_TILE)
                     add_bias_and_store(b, j, sums, 0)
                     quantise_wo(first)
                     add_bias_and_store(b, j, sums, 2)

@@ -25,7 +25,6 @@ HEADS = B * H
 WO_LOAD = 1024
 PAIRS = HEADS // 2
 AHEAD = 2
-PIECES = 4
 
 FLOPS = 2 * B * H * S * DH * DH + 2 * B * S * HID * E
 
@@ -94,9 +93,8 @@ def tile_linearattention_pb_kernel(tc, q_feat, kv, denom, Wo, bo, out):
                 load_kv(u)
             if u in (3, 4, 5):
                 load_wo(0, u - 3)
-            if u == 4:
-                nc.sync.dma_start(out=bias_sb[:], in_=bo.partition_broadcast(P))
         load_wo(0, 3)
+        nc.sync.dma_start(out=bias_sb[:], in_=bo.partition_broadcast(P))
         ident = keep.tile([P, P], BF16, name="ident")
         make_identity(nc, ident[:])
         ident_w = keep.tile([P, P], F32, name="ident_w")
@@ -124,7 +122,7 @@ def tile_linearattention_pb_kernel(tc, q_feat, kv, denom, Wo, bo, out):
                         qT_ps[:, tt, i, :], q_sb[u // 2][:, slot + tt, i * DH : (i + 1) * DH], ident[:]
                     )
             qT = qt_pool.tile([P, 2, ROW_TILES, P], BF16, name="qT")
-            nc.scalar.copy(out=qT[:], in_=qT_ps[:])
+            nc.vector.tensor_copy(out=qT[:], in_=qT_ps[:])
             qT_tiles.append(qT)
 
         def multiply_head(n):
@@ -144,12 +142,7 @@ def tile_linearattention_pb_kernel(tc, q_feat, kv, denom, Wo, bo, out):
                 )
             dst = c_tiles[u][:, :, :, t * (DH // 2) : (t + 1) * (DH // 2)]
             scale = rden[:, n : n + 1]
-            if t % 2 == 0:
-                nc.vector.tensor_scalar(
-                    out=dst, in0=ps[:], scalar1=scale, scalar2=None, op0=mybir.AluOpType.mult
-                )
-            else:
-                nc.scalar.activation(out=dst, in_=ps[:], func=COPY, scale=scale)
+            nc.scalar.activation(out=dst, in_=ps[:], func=COPY, scale=scale)
 
         def turn_back(u, half):
             if half == 0:
@@ -177,22 +170,16 @@ def tile_linearattention_pb_kernel(tc, q_feat, kv, denom, Wo, bo, out):
                 in_=ctx_grouped[u][:].rearrange("p s t -> p (s t)"),
             )
 
-        def regroup(copy, w, c0, c1, on_gpsimd=False):
+        def regroup(copy, w, c0, c1):
             j, g = divmod(w, PASSES)
             if c0 == 0:
                 wo_grouped[w] = grouped_pool.tile(
                     [P, N_TILE, PACK], BF16, name="grouped", tag="grouped", align_bytes=64
                 )
             half, col = divmod(j * N_TILE, WO_LOAD)
-            extra = {}
-            if on_gpsimd:
-                extra = {"scalar1": 1.0, "scalar2": 0.0, "op0": mybir.AluOpType.mult, "op1": mybir.AluOpType.add}
             dst = wo_grouped[w][:, c0:c1, :].rearrange("p (c r) t -> p c t r", r=4)
             src = wo_raw[half, g][:, :, col + c0 : col + c1].rearrange("p t (c r) -> p c t r", r=4)
-            if on_gpsimd:
-                copy(dst, src, **extra)
-            else:
-                copy(out=dst, in_=src)
+            copy(out=dst, in_=src)
 
         def quantise_wo(w):
             nc.vector.quantize_mx(
@@ -233,11 +220,6 @@ def tile_linearattention_pb_kernel(tc, q_feat, kv, denom, Wo, bo, out):
             out_rows = out[b].rearrange("(p i) n -> p i n", i=ROW_TILES)
             nc.sync.dma_start(out=out_rows[:, i0 : i0 + 2, cols], in_=res[:])
 
-        for w in range(PASSES):
-            for piece in range(PIECES):
-                regroup(
-                    nc.gpsimd.tensor_scalar, w, piece * N_TILE // PIECES, (piece + 1) * N_TILE // PIECES, True
-                )
         for m in range(AHEAD):
             transpose_pair(m)
         for m in range(PAIRS):
@@ -250,16 +232,22 @@ def tile_linearattention_pb_kernel(tc, q_feat, kv, denom, Wo, bo, out):
                 turn_back(u - 1, second)
             if u >= 2 and second == 0:
                 quantise_ctx(u - 2)
-            if u in (5, 6, 7) and second == 1:
-                quantise_wo(u - 5)
+            if u >= 3 and second == 1:
+                w, part = divmod(u - 3, 2)
+                regroup(nc.vector.tensor_copy, w, part * N_TILE // 2, (part + 1) * N_TILE // 2)
+                if u in (5, 7):
+                    quantise_wo((u - 5) // 2)
         for g in range(PASSES):
             load_wo(1, g)
+        regroup(nc.scalar.copy, 3, 0, N_TILE)
+        regroup(nc.vector.tensor_copy, 2, N_TILE // 2, N_TILE)
         sums = new_sums(0)
         for i in range(ROW_TILES):
             one_pass(0, 0, sums, 0, i)
+        quantise_ctx(GROUPS - 2)
+        quantise_wo(2)
         turn_back(GROUPS - 1, 0)
         turn_back(GROUPS - 1, 1)
-        quantise_ctx(GROUPS - 2)
         quantise_wo(3)
         quantise_ctx(GROUPS - 1)
 

@@ -53,6 +53,7 @@ def tile_linearattention_pb_kernel(tc, q_feat, kv, denom, Wo, bo, out):
         bias_sb = keep.tile([P, E], BF16, name="bias_sb")
 
         kv_sb = [keep.tile([P, H, DH], BF16, name="kv_sb%d" % b) for b in range(B)]
+        kv_turned = [keep.tile([P, H, 2, DH // 2], BF16, name="kv_turned%d" % b) for b in range(B)]
         q_sb = []
 
         def load_q(u, t0, count):
@@ -112,6 +113,16 @@ def tile_linearattention_pb_kernel(tc, q_feat, kv, denom, Wo, bo, out):
         ctx_grouped = []
         wo_grouped = {}
 
+        def turn_kv(u):
+            b, g = divmod(u, PASSES)
+            heads = slice(PACK * g, PACK * (g + 1))
+            src = kv_sb[b][:, heads, :].rearrange("d h e -> d (h e)").bitcast(F32)
+            dst = kv_turned[b][:, heads, :, :].rearrange("d h u k -> d (h u k)").bitcast(F32)
+            nc.vector.tensor_copy(
+                out=dst.rearrange("d (h u p) -> d h u p", h=PACK, u=2),
+                in_=src.rearrange("d (h p u) -> d h u p", h=PACK, u=2),
+            )
+
         def transpose_pair(m):
             u, t = divmod(2 * m, PACK)
             slot = PACK * (u % 2) + t
@@ -134,9 +145,9 @@ def tile_linearattention_pb_kernel(tc, q_feat, kv, denom, Wo, bo, out):
             ps = psum_m.tile([P, ROW_TILES, 2, DH // 2], F32, name="ps", tag="m")
             for i in range(ROW_TILES):
                 nc.tensor.matmul(
-                    ps[:, i, :, :].rearrange("s u (p e) -> s p u e", e=2),
+                    ps[:, i, :, :].rearrange("s u k -> s (u k)"),
                     lhsT=qT_tiles[n // 2][:, n % 2, i, :],
-                    rhs=kv_sb[b][:, h, :].rearrange("d (p u e) -> d p u e", u=2, e=2),
+                    rhs=kv_turned[b][:, h, :, :].rearrange("d u k -> d (u k)"),
                     start=True,
                     stop=True,
                 )
@@ -220,11 +231,14 @@ def tile_linearattention_pb_kernel(tc, q_feat, kv, denom, Wo, bo, out):
             out_rows = out[b].rearrange("(p i) n -> p i n", i=ROW_TILES)
             nc.sync.dma_start(out=out_rows[:, i0 : i0 + 2, cols], in_=res[:])
 
+        turn_kv(0)
         for m in range(AHEAD):
             transpose_pair(m)
         for m in range(PAIRS):
             if m + AHEAD < PAIRS:
                 transpose_pair(m + AHEAD)
+            if m % 2 == 0 and m // 2 + 1 < GROUPS:
+                turn_kv(m // 2 + 1)
             multiply_head(2 * m)
             multiply_head(2 * m + 1)
             u, second = divmod(m, 2)

@@ -73,13 +73,18 @@ def tile_linearattention_pb_kernel(tc, q_feat, kv, denom, Wo, bo, out):
         wo_rows = Wo.rearrange("(g p t) n -> g p t n", p=P, t=PACK)
         wo_raw = {}
 
-        def load_wo(half, g):
-            if half == 0:
-                raw = keep.tile([P, PACK, WO_LOAD], BF16, name="wo_raw%d" % g)
-            else:
-                raw = early_pool.tile([P, PACK, WO_LOAD], BF16, name="wo_raw", tag="early")
-            nc.sync.dma_start(out=raw[:], in_=wo_rows[g, :, :, half * WO_LOAD : (half + 1) * WO_LOAD])
-            wo_raw[half, g] = raw
+        for g in range(PASSES):
+            wo_raw[0, g] = keep.tile([P, PACK, WO_LOAD], BF16, name="wo_raw%d" % g)
+
+        def load_wo_unit(w):
+            j, g = divmod(w, PASSES)
+            cols = slice(j * N_TILE, (j + 1) * N_TILE)
+            nc.sync.dma_start(out=wo_raw[0, g][:, :, cols], in_=wo_rows[g, :, :, cols])
+
+        def load_wo_half(g):
+            raw = early_pool.tile([P, PACK, WO_LOAD], BF16, name="wo_raw", tag="early")
+            nc.sync.dma_start(out=raw[:], in_=wo_rows[g, :, :, WO_LOAD:])
+            wo_raw[1, g] = raw
 
         for u in range(GROUPS):
             if u % 2 == 0:
@@ -92,10 +97,10 @@ def tile_linearattention_pb_kernel(tc, q_feat, kv, denom, Wo, bo, out):
             else:
                 load_q(u, 0, PACK)
                 load_kv(u)
-            if u in (3, 4, 5):
-                load_wo(0, u - 3)
-        load_wo(0, 3)
-        nc.sync.dma_start(out=bias_sb[:], in_=bo.partition_broadcast(P))
+            if u >= 4:
+                load_wo_unit(u - 4)
+        for w in range(PASSES, 2 * PASSES):
+            load_wo_unit(w)
         ident = keep.tile([P, P], BF16, name="ident")
         make_identity(nc, ident[:])
         ident_w = keep.tile([P, P], F32, name="ident_w")
@@ -251,8 +256,10 @@ def tile_linearattention_pb_kernel(tc, q_feat, kv, denom, Wo, bo, out):
                 regroup(nc.vector.tensor_copy, w, part * N_TILE // 2, (part + 1) * N_TILE // 2)
                 if u in (5, 7):
                     quantise_wo((u - 5) // 2)
-        for g in range(PASSES):
-            load_wo(1, g)
+        load_wo_half(0)
+        nc.sync.dma_start(out=bias_sb[:], in_=bo.partition_broadcast(P))
+        for g in range(1, PASSES):
+            load_wo_half(g)
         regroup(nc.scalar.copy, 3, 0, N_TILE)
         regroup(nc.vector.tensor_copy, 2, N_TILE // 2, N_TILE)
         sums = new_sums(0)

@@ -23,8 +23,6 @@ N_CHUNKS = E // N_TILE
 GROUPS = B * PASSES
 HEADS = B * H
 WO_LOAD = 1024
-PAIRS = HEADS // 2
-AHEAD = 2
 
 FLOPS = 2 * B * H * S * DH * DH + 2 * B * S * HID * E
 
@@ -35,7 +33,7 @@ def tile_linearattention_pb_kernel(tc, q_feat, kv, denom, Wo, bo, out):
         stack.enter_context(tc.manual_schedule())
         keep = stack.enter_context(tc.tile_pool(name="keep", bufs=1))
         early_pool = stack.enter_context(tc.tile_pool(name="early", bufs=GROUPS // 2))
-        qt_pool = stack.enter_context(tc.tile_pool(name="qt", bufs=AHEAD + 2))
+        qt_pool = stack.enter_context(tc.tile_pool(name="qt", bufs=5))
         c_pool = stack.enter_context(tc.tile_pool(name="c", bufs=3))
         grouped_pool = stack.enter_context(tc.tile_pool(name="grouped", bufs=7))
         res_pool = stack.enter_context(tc.tile_pool(name="res", bufs=8))
@@ -53,7 +51,6 @@ def tile_linearattention_pb_kernel(tc, q_feat, kv, denom, Wo, bo, out):
         bias_sb = keep.tile([P, E], BF16, name="bias_sb")
 
         kv_sb = [keep.tile([P, H, DH], BF16, name="kv_sb%d" % b) for b in range(B)]
-        kv_turned = [keep.tile([P, H, 2, DH // 2], BF16, name="kv_turned%d" % b) for b in range(B)]
         q_sb = []
 
         def load_q(u, t0, count):
@@ -73,18 +70,17 @@ def tile_linearattention_pb_kernel(tc, q_feat, kv, denom, Wo, bo, out):
         wo_rows = Wo.rearrange("(g p t) n -> g p t n", p=P, t=PACK)
         wo_raw = {}
 
-        for g in range(PASSES):
-            wo_raw[0, g] = keep.tile([P, PACK, WO_LOAD], BF16, name="wo_raw%d" % g)
-
         def load_wo_unit(w):
             j, g = divmod(w, PASSES)
-            cols = slice(j * N_TILE, (j + 1) * N_TILE)
-            nc.sync.dma_start(out=wo_raw[0, g][:, :, cols], in_=wo_rows[g, :, :, cols])
+            raw = keep.tile([P, PACK, N_TILE], BF16, name="wo_raw%d" % w)
+            nc.sync.dma_start(out=raw[:], in_=wo_rows[g, :, :, j * N_TILE : (j + 1) * N_TILE])
+            wo_raw[w] = raw[:]
 
         def load_wo_half(g):
             raw = early_pool.tile([P, PACK, WO_LOAD], BF16, name="wo_raw", tag="early")
             nc.sync.dma_start(out=raw[:], in_=wo_rows[g, :, :, WO_LOAD:])
-            wo_raw[1, g] = raw
+            for jj in range(2):
+                wo_raw[(2 + jj) * PASSES + g] = raw[:, :, jj * N_TILE : (jj + 1) * N_TILE]
 
         for u in range(GROUPS):
             if u % 2 == 0:
@@ -118,16 +114,6 @@ def tile_linearattention_pb_kernel(tc, q_feat, kv, denom, Wo, bo, out):
         ctx_grouped = []
         wo_grouped = {}
 
-        def turn_kv(u):
-            b, g = divmod(u, PASSES)
-            heads = slice(PACK * g, PACK * (g + 1))
-            src = kv_sb[b][:, heads, :].rearrange("d h e -> d (h e)").bitcast(F32)
-            dst = kv_turned[b][:, heads, :, :].rearrange("d h u k -> d (h u k)").bitcast(F32)
-            nc.vector.tensor_copy(
-                out=dst.rearrange("d (h u p) -> d h u p", h=PACK, u=2),
-                in_=src.rearrange("d (h p u) -> d h u p", h=PACK, u=2),
-            )
-
         def transpose_pair(m):
             u, t = divmod(2 * m, PACK)
             slot = PACK * (u % 2) + t
@@ -150,9 +136,9 @@ def tile_linearattention_pb_kernel(tc, q_feat, kv, denom, Wo, bo, out):
             ps = psum_m.tile([P, ROW_TILES, 2, DH // 2], F32, name="ps", tag="m")
             for i in range(ROW_TILES):
                 nc.tensor.matmul(
-                    ps[:, i, :, :].rearrange("s u k -> s (u k)"),
+                    ps[:, i, :, :].rearrange("s u (p e) -> s p u e", e=2),
                     lhsT=qT_tiles[n // 2][:, n % 2, i, :],
-                    rhs=kv_turned[b][:, h, :, :].rearrange("d u k -> d (u k)"),
+                    rhs=kv_sb[b][:, h, :].rearrange("d (p u e) -> d p u e", u=2, e=2),
                     start=True,
                     stop=True,
                 )
@@ -187,14 +173,12 @@ def tile_linearattention_pb_kernel(tc, q_feat, kv, denom, Wo, bo, out):
             )
 
         def regroup(copy, w, c0, c1):
-            j, g = divmod(w, PASSES)
             if c0 == 0:
                 wo_grouped[w] = grouped_pool.tile(
                     [P, N_TILE, PACK], BF16, name="grouped", tag="grouped", align_bytes=64
                 )
-            half, col = divmod(j * N_TILE, WO_LOAD)
             dst = wo_grouped[w][:, c0:c1, :].rearrange("p (c r) t -> p c t r", r=4)
-            src = wo_raw[half, g][:, :, col + c0 : col + c1].rearrange("p t (c r) -> p c t r", r=4)
+            src = wo_raw[w][:, :, c0:c1].rearrange("p t (c r) -> p c t r", r=4)
             copy(out=dst, in_=src)
 
         def quantise_wo(w):
@@ -236,22 +220,24 @@ def tile_linearattention_pb_kernel(tc, q_feat, kv, denom, Wo, bo, out):
             out_rows = out[b].rearrange("(p i) n -> p i n", i=ROW_TILES)
             nc.sync.dma_start(out=out_rows[:, i0 : i0 + 2, cols], in_=res[:])
 
-        turn_kv(0)
-        for m in range(AHEAD):
-            transpose_pair(m)
-        for m in range(PAIRS):
-            if m + AHEAD < PAIRS:
-                transpose_pair(m + AHEAD)
-            if m % 2 == 0 and m // 2 + 1 < GROUPS:
-                turn_kv(m // 2 + 1)
-            multiply_head(2 * m)
-            multiply_head(2 * m + 1)
-            u, second = divmod(m, 2)
+        transpose_pair(0)
+        transpose_pair(1)
+        for u in range(GROUPS):
+            if u + 1 < GROUPS:
+                transpose_pair(2 * u + 2)
+            if u == 0:
+                multiply_head(0)
+                multiply_head(1)
+            if u + 1 < GROUPS:
+                transpose_pair(2 * u + 3)
+            for n in range(PACK * u + (2 if u == 0 else 0), PACK * (u + 1)):
+                multiply_head(n)
             if u >= 1:
-                turn_back(u - 1, second)
-            if u >= 2 and second == 0:
+                turn_back(u - 1, 0)
+                turn_back(u - 1, 1)
+            if u >= 2:
                 quantise_ctx(u - 2)
-            if u >= 3 and second == 1:
+            if u >= 3:
                 w, part = divmod(u - 3, 2)
                 regroup(nc.vector.tensor_copy, w, part * N_TILE // 2, (part + 1) * N_TILE // 2)
                 if u in (5, 7):

@@ -22,6 +22,7 @@ N_TILE = 512
 N_CHUNKS = E // N_TILE
 GROUPS = B * PASSES
 HEADS = B * H
+WARM_UP = 14
 WO_LOAD = 1024
 
 FLOPS = 2 * B * H * S * DH * DH + 2 * B * S * HID * E
@@ -33,21 +34,17 @@ def tile_linearattention_pb_kernel(tc, q_feat, kv, denom, Wo, bo, out):
         stack.enter_context(tc.manual_schedule())
         keep = stack.enter_context(tc.tile_pool(name="keep", bufs=1))
         early_pool = stack.enter_context(tc.tile_pool(name="early", bufs=GROUPS // 2))
-        qt_pool = stack.enter_context(tc.tile_pool(name="qt", bufs=5))
+        qt_pool = stack.enter_context(tc.tile_pool(name="qt", bufs=4))
         c_pool = stack.enter_context(tc.tile_pool(name="c", bufs=3))
-        grouped_pool = stack.enter_context(tc.tile_pool(name="grouped", bufs=7))
+        grouped_pool = stack.enter_context(tc.tile_pool(name="grouped", bufs=9))
         res_pool = stack.enter_context(tc.tile_pool(name="res", bufs=8))
         psum_t = stack.enter_context(tc.psum_pool(name="psum_t", bufs=2))
         psum_r = stack.enter_context(tc.psum_pool(name="psum_r", bufs=2))
         psum_m = stack.enter_context(tc.psum_pool(name="psum_m", bufs=4))
 
         den_bf = keep.tile([P, HEADS], BF16, name="den_bf")
-        nc.scalar.dma_start(
-            out=den_bf[:], in_=denom.rearrange("b h x y -> (b h x y)").partition_broadcast(P)
-        )
         dummy = keep.tile([P, 2], F32, name="dummy")
         nc.vector.memset(dummy[:], 1.0)
-        nc.scalar.copy(out=dummy[:, 1:2], in_=dummy[:, 0:1])
         bias_sb = keep.tile([P, E], BF16, name="bias_sb")
 
         kv_sb = [keep.tile([P, H, DH], BF16, name="kv_sb%d" % b) for b in range(B)]
@@ -65,7 +62,8 @@ def tile_linearattention_pb_kernel(tc, q_feat, kv, denom, Wo, bo, out):
         def load_kv(u):
             b, g = divmod(u, PASSES)
             heads = slice(PACK * g, PACK * (g + 1))
-            nc.sync.dma_start(out=kv_sb[b][:, heads, :], in_=kv[b, heads].rearrange("t d e -> d t e"))
+            queue = nc.scalar if u == 0 else nc.sync
+            queue.dma_start(out=kv_sb[b][:, heads, :], in_=kv[b, heads].rearrange("t d e -> d t e"))
 
         wo_rows = Wo.rearrange("(g p t) n -> g p t n", p=P, t=PACK)
         wo_raw = {}
@@ -89,14 +87,19 @@ def tile_linearattention_pb_kernel(tc, q_feat, kv, denom, Wo, bo, out):
             if u == 0:
                 load_q(u, 0, 2)
                 load_kv(u)
+                nc.scalar.dma_start(
+                    out=den_bf[:], in_=denom.rearrange("b h x y -> (b h x y)").partition_broadcast(P)
+                )
                 load_q(u, 2, 2)
             else:
                 load_q(u, 0, PACK)
                 load_kv(u)
             if u >= 4:
                 load_wo_unit(u - 4)
+        nc.sync.dma_start(out=bias_sb[:], in_=bo.partition_broadcast(P))
         for w in range(PASSES, 2 * PASSES):
             load_wo_unit(w)
+        nc.scalar.copy(out=dummy[:, 1:2], in_=dummy[:, 0:1])
         ident = keep.tile([P, P], BF16, name="ident")
         make_identity(nc, ident[:])
         ident_w = keep.tile([P, P], F32, name="ident_w")
@@ -144,9 +147,14 @@ def tile_linearattention_pb_kernel(tc, q_feat, kv, denom, Wo, bo, out):
                 )
             dst = c_tiles[u][:, :, :, t * (DH // 2) : (t + 1) * (DH // 2)]
             scale = rden[:, n : n + 1]
-            nc.scalar.activation(out=dst, in_=ps[:], func=COPY, scale=scale)
+            if t == 1 and u in (1, 3, 5):
+                nc.vector.tensor_scalar(
+                    out=dst, in0=ps[:], scalar1=scale, scalar2=None, op0=mybir.AluOpType.mult
+                )
+            else:
+                nc.scalar.activation(out=dst, in_=ps[:], func=COPY, scale=scale)
 
-        def turn_back(u, half):
+        def turn_back(u, half, on_scalar=False):
             if half == 0:
                 ctx_grouped.append(
                     grouped_pool.tile([P, S, PACK], BF16, name="grouped", tag="grouped", align_bytes=64)
@@ -159,7 +167,7 @@ def tile_linearattention_pb_kernel(tc, q_feat, kv, denom, Wo, bo, out):
                     nc.tensor.transpose(back[:, ii, w, :], words[:, first : first + P], ident_w[:])
             dst = ctx_grouped[u][:].rearrange("p s t -> p (s t)").bitcast(F32)
             width = S * 2 // 2
-            copy = nc.vector.tensor_copy if half == 0 else nc.scalar.copy
+            copy = nc.scalar.copy if on_scalar else nc.vector.tensor_copy
             copy(
                 out=dst[:, half * width : (half + 1) * width].rearrange("p (i s w) -> p i s w", i=2, w=2),
                 in_=back[:].rearrange("p i w s -> p i s w"),
@@ -192,19 +200,19 @@ def tile_linearattention_pb_kernel(tc, q_feat, kv, denom, Wo, bo, out):
             if b == 0:
                 homes = [(psum_m, "m")] * ROW_TILES
             else:
-                homes = [(psum_t, "t"), (psum_r, "r")] * 2
+                homes = [(psum_t, "t")] * 2 + [(psum_r, "r")] * 2
             return [pool.tile([P, N_TILE], F32, name="sums", tag=tag) for pool, tag in homes]
 
-        def one_pass(b, j, sums, g, i):
+        def one_pass(b, j, bank, g, i, cols=slice(0, N_TILE)):
             u = b * PASSES + g
             w = j * PASSES + g
             rows = slice(i * P, (i + 1) * P)
             nc.tensor.matmul_mx(
-                out=sums[i][:],
+                out=bank[:, cols],
                 lhsT=ctx_codes[:, u, rows].bitcast(FP8X4),
                 lhsT_scale=ctx_scales[:, u, rows],
-                rhs=wo_codes[:, w, :].bitcast(FP8X4),
-                rhs_scale=wo_scales[:, w, :],
+                rhs=wo_codes[:, w, cols].bitcast(FP8X4),
+                rhs_scale=wo_scales[:, w, cols],
                 start=(g == 0),
                 stop=(g == PASSES - 1),
             )
@@ -220,6 +228,29 @@ def tile_linearattention_pb_kernel(tc, q_feat, kv, denom, Wo, bo, out):
             out_rows = out[b].rearrange("(p i) n -> p i n", i=ROW_TILES)
             nc.sync.dma_start(out=out_rows[:, i0 : i0 + 2, cols], in_=res[:])
 
+        def finish(b, j):
+            out_rows = out[b].rearrange("(p i) n -> p i n", i=ROW_TILES)
+            whole = slice(0, N_TILE)
+            halves = [slice(0, N_TILE // 2), slice(N_TILE // 2, N_TILE)]
+            banks = new_sums(b)
+            parts = [(i, whole, banks[i]) for i in range(ROW_TILES - 1)]
+            spare = psum_m.tile([P, N_TILE], F32, name="sums", tag="m")
+            parts += [(ROW_TILES - 1, halves[0], banks[ROW_TILES - 1]), (ROW_TILES - 1, halves[1], spare)]
+            for i, cols, bank in parts:
+                for g in range(PASSES):
+                    one_pass(b, j, bank, g, i, cols)
+                width = cols.stop - cols.start
+                first = j * N_TILE + cols.start
+                res = res_pool.tile([P, 2, N_TILE], F32, name="res", align_bytes=64)
+                nc.vector.tensor_tensor(
+                    out=res[:, 0, 0:width], in0=bank[:, cols], in1=bias_sb[:, first : first + width],
+                    op=mybir.AluOpType.add,
+                )
+                nc.sync.dma_start(out=out_rows[:, i, first : first + width], in_=res[:, 0, 0:width])
+
+        warm = psum_m.tile([P, P], F32, name="warm", tag="m")
+        for n in range(WARM_UP):
+            nc.tensor.matmul(warm[:], lhsT=ident[:], rhs=ident[:], start=True, stop=True)
         transpose_pair(0)
         transpose_pair(1)
         for u in range(GROUPS):
@@ -232,44 +263,60 @@ def tile_linearattention_pb_kernel(tc, q_feat, kv, denom, Wo, bo, out):
                 transpose_pair(2 * u + 3)
             for n in range(PACK * u + (2 if u == 0 else 0), PACK * (u + 1)):
                 multiply_head(n)
+            if u >= 4:
+                w, part = divmod(u - 4, 2)
+                regroup(nc.vector.tensor_copy, w, part * N_TILE // 2, (part + 1) * N_TILE // 2)
+            if u == 6:
+                quantise_wo(0)
             if u >= 1:
                 turn_back(u - 1, 0)
-                turn_back(u - 1, 1)
-            if u >= 2:
+                turn_back(u - 1, 1, on_scalar=True)
+            if 2 <= u <= PASSES + 2:
                 quantise_ctx(u - 2)
-            if u >= 3:
-                w, part = divmod(u - 3, 2)
-                regroup(nc.vector.tensor_copy, w, part * N_TILE // 2, (part + 1) * N_TILE // 2)
-                if u in (5, 7):
-                    quantise_wo((u - 5) // 2)
-        load_wo_half(0)
-        nc.sync.dma_start(out=bias_sb[:], in_=bo.partition_broadcast(P))
-        for g in range(1, PASSES):
+        for g in range(PASSES):
             load_wo_half(g)
-        regroup(nc.scalar.copy, 3, 0, N_TILE)
-        regroup(nc.vector.tensor_copy, 2, N_TILE // 2, N_TILE)
-        sums = new_sums(0)
+
+        sums = [new_sums(0), None]
+        regroup(nc.scalar.copy, 2, 0, N_TILE)
+        quantise_wo(1)
         for i in range(ROW_TILES):
-            one_pass(0, 0, sums, 0, i)
-        quantise_ctx(GROUPS - 2)
-        quantise_wo(2)
+            one_pass(0, 0, sums[0][i], 0, i)
         turn_back(GROUPS - 1, 0)
         turn_back(GROUPS - 1, 1)
+        sums[1] = new_sums(1)
+        for i in range(ROW_TILES):
+            one_pass(1, 0, sums[1][i], 0, i)
+        for w in (3, 5, 6, 7):
+            regroup(nc.scalar.copy, w, 0, N_TILE)
+        quantise_ctx(PASSES + 1)
+        quantise_wo(2)
+        quantise_ctx(PASSES + 2)
+        quantise_ctx(PASSES + 3)
+        regroup(nc.vector.tensor_copy, 4, 0, N_TILE // 2)
         quantise_wo(3)
-        quantise_ctx(GROUPS - 1)
-
-        for j in range(N_CHUNKS):
+        regroup(nc.vector.tensor_copy, 4, N_TILE // 2, N_TILE)
+        for g in range(1, PASSES):
             for b in range(B):
-                if (j, b) == (0, 0):
-                    order = [(g, i) for g in range(1, PASSES) for i in range(ROW_TILES)]
-                elif (j, b) != (N_CHUNKS - 1, B - 1):
-                    sums = new_sums(b)
-                    order = [(g, i) for g in range(PASSES) for i in range(ROW_TILES)]
-                else:
-                    sums = new_sums(b)
-                    order = [(g, i) for i in range(ROW_TILES) for g in range(PASSES)]
-                for g, i in order:
-                    one_pass(b, j, sums, g, i)
+                for i in range(ROW_TILES):
+                    one_pass(b, 0, sums[b][i], g, i)
+        quantise_wo(5)
+        quantise_wo(4)
+        add_bias_and_store(0, 0, sums[0], 0)
+        add_bias_and_store(0, 0, sums[0], 2)
+        quantise_wo(6)
+        add_bias_and_store(1, 0, sums[1], 0)
+        quantise_wo(7)
+        add_bias_and_store(1, 0, sums[1], 2)
+
+        for j in range(1, N_CHUNKS):
+            for b in range(B):
+                if (j, b) == (N_CHUNKS - 1, B - 1):
+                    finish(b, j)
+                    continue
+                sums = new_sums(b)
+                for g in range(PASSES):
+                    for i in range(ROW_TILES):
+                        one_pass(b, j, sums[i], g, i)
                 first = (j + 1) * PASSES
                 more = j + 1 < N_CHUNKS
                 if more and b == 0:

@@ -123,9 +123,11 @@ def tile_linearattention_pb_kernel(tc, q_feat, kv, denom, Wo, bo, out):
             qT_ps = psum_t.tile([P, 2, ROW_TILES, P], BF16, name="qT_ps", tag="t")
             for tt in range(2):
                 for i in range(ROW_TILES):
-                    nc.tensor.transpose(
-                        qT_ps[:, tt, i, :], q_sb[u // 2][:, slot + tt, i * DH : (i + 1) * DH], ident[:]
-                    )
+                    rows = q_sb[u // 2][:, slot + tt, i * DH : (i + 1) * DH]
+                    if m % 2 == 0:
+                        nc.tensor.transpose(qT_ps[:, tt, i, :], rows, ident[:])
+                    else:
+                        nc.tensor.matmul(qT_ps[:, tt, i, :], lhsT=rows, rhs=ident[:], start=True, stop=True)
             qT = qt_pool.tile([P, 2, ROW_TILES, P], BF16, name="qT")
             nc.vector.tensor_copy(out=qT[:], in_=qT_ps[:])
             qT_tiles.append(qT)

@@ -23,6 +23,7 @@ N_CHUNKS = E // N_TILE
 GROUPS = B * PASSES
 HEADS = B * H
 WARM_UP = 14
+PIECES = 8
 WO_LOAD = 1024
 
 FLOPS = 2 * B * H * S * DH * DH + 2 * B * S * HID * E
@@ -124,7 +125,7 @@ def tile_linearattention_pb_kernel(tc, q_feat, kv, denom, Wo, bo, out):
             for tt in range(2):
                 for i in range(ROW_TILES):
                     rows = q_sb[u // 2][:, slot + tt, i * DH : (i + 1) * DH]
-                    if m % 2 == 0:
+                    if t + tt == 0:
                         nc.tensor.transpose(qT_ps[:, tt, i, :], rows, ident[:])
                     else:
                         nc.tensor.matmul(qT_ps[:, tt, i, :], lhsT=rows, rhs=ident[:], start=True, stop=True)
@@ -149,7 +150,7 @@ def tile_linearattention_pb_kernel(tc, q_feat, kv, denom, Wo, bo, out):
                 )
             dst = c_tiles[u][:, :, :, t * (DH // 2) : (t + 1) * (DH // 2)]
             scale = rden[:, n : n + 1]
-            if t == 1 and u in (1, 3, 5):
+            if t == 1 and u in (1, 3, 5, 6, 7):
                 nc.vector.tensor_scalar(
                     out=dst, in0=ps[:], scalar1=scale, scalar2=None, op0=mybir.AluOpType.mult
                 )
@@ -190,6 +191,18 @@ def tile_linearattention_pb_kernel(tc, q_feat, kv, denom, Wo, bo, out):
             dst = wo_grouped[w][:, c0:c1, :].rearrange("p (c r) t -> p c t r", r=4)
             src = wo_raw[w][:, :, c0:c1].rearrange("p t (c r) -> p c t r", r=4)
             copy(out=dst, in_=src)
+
+        def regroup_on_gpsimd(w):
+            wo_grouped[w] = grouped_pool.tile(
+                [P, N_TILE, PACK], BF16, name="grouped", tag="grouped", align_bytes=64
+            )
+            width = N_TILE // PIECES
+            for c0 in range(0, N_TILE, width):
+                nc.gpsimd.tensor_scalar(
+                    out=wo_grouped[w][:, c0 : c0 + width, :].rearrange("p (c r) t -> p c t r", r=4),
+                    in0=wo_raw[w][:, :, c0 : c0 + width].rearrange("p t (c r) -> p c t r", r=4),
+                    scalar1=1.0, scalar2=0.0, op0=mybir.AluOpType.mult, op1=mybir.AluOpType.add,
+                )
 
         def quantise_wo(w):
             nc.vector.quantize_mx(
@@ -253,6 +266,8 @@ def tile_linearattention_pb_kernel(tc, q_feat, kv, denom, Wo, bo, out):
         warm = psum_m.tile([P, P], F32, name="warm", tag="m")
         for n in range(WARM_UP):
             nc.tensor.matmul(warm[:], lhsT=ident[:], rhs=ident[:], start=True, stop=True)
+        regroup_on_gpsimd(0)
+        regroup_on_gpsimd(1)
         transpose_pair(0)
         transpose_pair(1)
         for u in range(GROUPS):
@@ -265,9 +280,6 @@ def tile_linearattention_pb_kernel(tc, q_feat, kv, denom, Wo, bo, out):
                 transpose_pair(2 * u + 3)
             for n in range(PACK * u + (2 if u == 0 else 0), PACK * (u + 1)):
                 multiply_head(n)
-            if u >= 4:
-                w, part = divmod(u - 4, 2)
-                regroup(nc.vector.tensor_copy, w, part * N_TILE // 2, (part + 1) * N_TILE // 2)
             if u == 6:
                 quantise_wo(0)
             if u >= 1:

@@ -22,7 +22,7 @@ N_TILE = 512
 N_CHUNKS = E // N_TILE
 GROUPS = B * PASSES
 HEADS = B * H
-WARM_UP = 14
+WARM_UP = 12
 PIECES = 8
 WO_LOAD = 1024
 
@@ -106,7 +106,6 @@ def tile_linearattention_pb_kernel(tc, q_feat, kv, denom, Wo, bo, out):
         ident_w = keep.tile([P, P], F32, name="ident_w")
         make_identity(nc, ident_w[:])
         rden = keep.tile([P, HEADS], F32, name="rden")
-        nc.vector.reciprocal(out=rden[:], in_=den_bf[:])
 
         ctx_codes = keep.tile([P, GROUPS, S], U32, name="ctx_codes", align_bytes=64)
         ctx_scales = keep.tile([P, GROUPS, S], U8, name="ctx_scales", align_bytes=64)
@@ -130,7 +129,8 @@ def tile_linearattention_pb_kernel(tc, q_feat, kv, denom, Wo, bo, out):
                     else:
                         nc.tensor.matmul(qT_ps[:, tt, i, :], lhsT=rows, rhs=ident[:], start=True, stop=True)
             qT = qt_pool.tile([P, 2, ROW_TILES, P], BF16, name="qT")
-            nc.vector.tensor_copy(out=qT[:], in_=qT_ps[:])
+            copy = nc.scalar.copy if m == 1 else nc.vector.tensor_copy
+            copy(out=qT[:], in_=qT_ps[:])
             qT_tiles.append(qT)
 
         def multiply_head(n):
@@ -269,6 +269,7 @@ def tile_linearattention_pb_kernel(tc, q_feat, kv, denom, Wo, bo, out):
         regroup_on_gpsimd(0)
         regroup_on_gpsimd(1)
         transpose_pair(0)
+        nc.vector.reciprocal(out=rden[:], in_=den_bf[:])
         transpose_pair(1)
         for u in range(GROUPS):
             if u + 1 < GROUPS:
@@ -334,7 +335,8 @@ def tile_linearattention_pb_kernel(tc, q_feat, kv, denom, Wo, bo, out):
                 first = (j + 1) * PASSES
                 more = j + 1 < N_CHUNKS
                 if more and b == 0:
-                    regroup(nc.scalar.copy, first, 0, N_TILE)
+                    regroup(nc.vector.tensor_copy, first, 0, N_TILE // 2)
+                    regroup(nc.scalar.copy, first, N_TILE // 2, N_TILE)
                     regroup(nc.scalar.copy, first + 1, 0, N_TILE)
                     add_bias_and_store(b, j, sums, 0)
                     quantise_wo(first)

@@ -107,10 +107,16 @@ def tile_linearattention_pb_kernel(tc, q_feat, kv, denom, Wo, bo, out):
         make_identity(nc, ident_w[:])
         rden = keep.tile([P, HEADS], F32, name="rden")
 
-        ctx_codes = keep.tile([P, GROUPS, S], U32, name="ctx_codes", align_bytes=64)
-        ctx_scales = keep.tile([P, GROUPS, S], U8, name="ctx_scales", align_bytes=64)
-        wo_codes = keep.tile([P, N_CHUNKS * PASSES, N_TILE], U32, name="wo_codes", align_bytes=64)
-        wo_scales = keep.tile([P, N_CHUNKS * PASSES, N_TILE], U8, name="wo_scales", align_bytes=64)
+        ctx_words = GROUPS * S
+        wo_words = N_CHUNKS * PASSES * N_TILE
+        ctx_codes = keep.tile([P, ctx_words + 16], U32, name="ctx_codes", align_bytes=64)
+        ctx_codes = ctx_codes[:, 0:ctx_words].rearrange("p (u s) -> p u s", s=S)
+        ctx_scales = keep.tile([P, ctx_words + 64], U8, name="ctx_scales", align_bytes=64)
+        ctx_scales = ctx_scales[:, 0:ctx_words].rearrange("p (u s) -> p u s", s=S)
+        wo_codes = keep.tile([P, wo_words + 16], U32, name="wo_codes", align_bytes=64)
+        wo_codes = wo_codes[:, 0:wo_words].rearrange("p (w n) -> p w n", n=N_TILE)
+        wo_scales = keep.tile([P, wo_words], U8, name="wo_scales", align_bytes=64)
+        wo_scales = wo_scales[:].rearrange("p (w n) -> p w n", n=N_TILE)
 
         qT_tiles = []
         c_tiles = []

from contextlib import ExitStack

import concourse.mybir as mybir
from concourse.masks import make_identity

BF16 = mybir.dt.bfloat16
F32 = mybir.dt.float32
U32 = mybir.dt.uint32
U8 = mybir.dt.uint8
FP8X4 = mybir.dt.float8_e4m3fn_x4
COPY = mybir.ActivationFunctionType.Copy

B, H, S, DH = 2, 16, 512, 128
HID = H * DH
E = 2048

P = 128
PACK = 4
PASSES = HID // (P * PACK)
ROW_TILES = S // P
N_TILE = 512
N_CHUNKS = E // N_TILE
GROUPS = B * PASSES
HEADS = B * H
WARM_UP = 12
PIECES = 8
WO_LOAD = 1024

FLOPS = 2 * B * H * S * DH * DH + 2 * B * S * HID * E


def tile_linearattention_pb_kernel(tc, q_feat, kv, denom, Wo, bo, out):
    nc = tc.nc
    with ExitStack() as stack:
        stack.enter_context(tc.manual_schedule())
        keep = stack.enter_context(tc.tile_pool(name="keep", bufs=1))
        early_pool = stack.enter_context(tc.tile_pool(name="early", bufs=GROUPS // 2))
        qt_pool = stack.enter_context(tc.tile_pool(name="qt", bufs=4))
        c_pool = stack.enter_context(tc.tile_pool(name="c", bufs=3))
        grouped_pool = stack.enter_context(tc.tile_pool(name="grouped", bufs=9))
        res_pool = stack.enter_context(tc.tile_pool(name="res", bufs=8))
        psum_t = stack.enter_context(tc.psum_pool(name="psum_t", bufs=2))
        psum_r = stack.enter_context(tc.psum_pool(name="psum_r", bufs=2))
        psum_m = stack.enter_context(tc.psum_pool(name="psum_m", bufs=4))

        den_bf = keep.tile([P, HEADS], BF16, name="den_bf")
        dummy = keep.tile([P, 2], F32, name="dummy")
        nc.vector.memset(dummy[:], 1.0)
        bias_sb = keep.tile([P, E], BF16, name="bias_sb")

        kv_sb = [keep.tile([P, H, DH], BF16, name="kv_sb%d" % b) for b in range(B)]
        q_sb = []

        def load_q(u, t0, count):
            b, g = divmod(u, PASSES)
            heads = slice(PACK * g + t0, PACK * g + t0 + count)
            slot = PACK * (g % 2) + t0
            nc.sync.dma_start(
                out=q_sb[u // 2][:, slot : slot + count, :],
                in_=q_feat[b, heads].rearrange("t (p i) d -> p t (i d)", i=ROW_TILES),
            )

        def load_kv(u):
            b, g = divmod(u, PASSES)
            heads = slice(PACK * g, PACK * (g + 1))
            queue = nc.scalar if u == 0 else nc.sync
            queue.dma_start(out=kv_sb[b][:, heads, :], in_=kv[b, heads].rearrange("t d e -> d t e"))

        wo_rows = Wo.rearrange("(g p t) n -> g p t n", p=P, t=PACK)
        wo_raw = {}

        def load_wo_unit(w):
            j, g = divmod(w, PASSES)
            raw = keep.tile([P, PACK, N_TILE], BF16, name="wo_raw%d" % w)
            nc.sync.dma_start(out=raw[:], in_=wo_rows[g, :, :, j * N_TILE : (j + 1) * N_TILE])
            wo_raw[w] = raw[:]

        def load_wo_half(g):
            raw = early_pool.tile([P, PACK, WO_LOAD], BF16, name="wo_raw", tag="early")
            nc.sync.dma_start(out=raw[:], in_=wo_rows[g, :, :, WO_LOAD:])
            for jj in range(2):
                wo_raw[(2 + jj) * PASSES + g] = raw[:, :, jj * N_TILE : (jj + 1) * N_TILE]

        for u in range(GROUPS):
            if u % 2 == 0:
                q_pair = early_pool.tile([P, 2 * PACK, S], BF16, name="q_pair", tag="early")
                q_sb.append(q_pair)
            if u == 0:
                load_q(u, 0, 2)
                load_kv(u)
                nc.scalar.dma_start(
                    out=den_bf[:], in_=denom.rearrange("b h x y -> (b h x y)").partition_broadcast(P)
                )
                load_q(u, 2, 2)
            else:
                load_q(u, 0, PACK)
                load_kv(u)
            if u >= 4:
                load_wo_unit(u - 4)
        nc.sync.dma_start(out=bias_sb[:], in_=bo.partition_broadcast(P))
        for w in range(PASSES, 2 * PASSES):
            load_wo_unit(w)
        nc.scalar.copy(out=dummy[:, 1:2], in_=dummy[:, 0:1])
        ident = keep.tile([P, P], BF16, name="ident")
        make_identity(nc, ident[:])
        ident_w = keep.tile([P, P], F32, name="ident_w")
        make_identity(nc, ident_w[:])
        rden = keep.tile([P, HEADS], F32, name="rden")

        ctx_words = GROUPS * S
        wo_words = N_CHUNKS * PASSES * N_TILE
        ctx_codes = keep.tile([P, ctx_words + 16], U32, name="ctx_codes", align_bytes=64)
        ctx_codes = ctx_codes[:, 0:ctx_words].rearrange("p (u s) -> p u s", s=S)
        ctx_scales = keep.tile([P, ctx_words + 64], U8, name="ctx_scales", align_bytes=64)
        ctx_scales = ctx_scales[:, 0:ctx_words].rearrange("p (u s) -> p u s", s=S)
        wo_codes = keep.tile([P, wo_words + 16], U32, name="wo_codes", align_bytes=64)
        wo_codes = wo_codes[:, 0:wo_words].rearrange("p (w n) -> p w n", n=N_TILE)
        wo_scales = keep.tile([P, wo_words], U8, name="wo_scales", align_bytes=64)
        wo_scales = wo_scales[:].rearrange("p (w n) -> p w n", n=N_TILE)

        qT_tiles = []
        c_tiles = []
        ctx_grouped = []
        wo_grouped = {}

        def transpose_pair(m):
            u, t = divmod(2 * m, PACK)
            slot = PACK * (u % 2) + t
            qT_ps = psum_t.tile([P, 2, ROW_TILES, P], BF16, name="qT_ps", tag="t")
            for tt in range(2):
                for i in range(ROW_TILES):
                    rows = q_sb[u // 2][:, slot + tt, i * DH : (i + 1) * DH]
                    if t + tt == 0:
                        nc.tensor.transpose(qT_ps[:, tt, i, :], rows, ident[:])
                    else:
                        nc.tensor.matmul(qT_ps[:, tt, i, :], lhsT=rows, rhs=ident[:], start=True, stop=True)
            qT = qt_pool.tile([P, 2, ROW_TILES, P], BF16, name="qT")
            copy = nc.scalar.copy if m == 1 else nc.vector.tensor_copy
            copy(out=qT[:], in_=qT_ps[:])
            qT_tiles.append(qT)

        def multiply_head(n):
            u, t = divmod(n, PACK)
            b, g = divmod(u, PASSES)
            h = PACK * g + t
            if t == 0:
                c_tiles.append(c_pool.tile([P, ROW_TILES, 2, P * 2], BF16, name="c", align_bytes=64))
            ps = psum_m.tile([P, ROW_TILES, 2, DH // 2], F32, name="ps", tag="m")
            for i in range(ROW_TILES):
                nc.tensor.matmul(
                    ps[:, i, :, :].rearrange("s u (p e) -> s p u e", e=2),
                    lhsT=qT_tiles[n // 2][:, n % 2, i, :],
                    rhs=kv_sb[b][:, h, :].rearrange("d (p u e) -> d p u e", u=2, e=2),
                    start=True,
                    stop=True,
                )
            dst = c_tiles[u][:, :, :, t * (DH // 2) : (t + 1) * (DH // 2)]
            scale = rden[:, n : n + 1]
            if t == 1 and u in (1, 3, 5, 6, 7):
                nc.vector.tensor_scalar(
                    out=dst, in0=ps[:], scalar1=scale, scalar2=None, op0=mybir.AluOpType.mult
                )
            else:
                nc.scalar.activation(out=dst, in_=ps[:], func=COPY, scale=scale)

        def turn_back(u, half, on_scalar=False):
            if half == 0:
                ctx_grouped.append(
                    grouped_pool.tile([P, S, PACK], BF16, name="grouped", tag="grouped", align_bytes=64)
                )
            words = c_tiles[u][:].rearrange("s i u k -> s (i u k)").bitcast(F32)
            back = psum_r.tile([P, 2, 2, P], F32, name="back", tag="r")
            for ii in range(2):
                for w in range(2):
                    first = ((2 * half + ii) * 2 + w) * P
                    nc.tensor.transpose(back[:, ii, w, :], words[:, first : first + P], ident_w[:])
            dst = ctx_grouped[u][:].rearrange("p s t -> p (s t)").bitcast(F32)
            width = S * 2 // 2
            copy = nc.scalar.copy if on_scalar else nc.vector.tensor_copy
            copy(
                out=dst[:, half * width : (half + 1) * width].rearrange("p (i s w) -> p i s w", i=2, w=2),
                in_=back[:].rearrange("p i w s -> p i s w"),
            )

        def quantise_ctx(u):
            nc.vector.quantize_mx(
                out=ctx_codes[:, u, :].bitcast(FP8X4),
                scales=ctx_scales[:, u, :],
                in_=ctx_grouped[u][:].rearrange("p s t -> p (s t)"),
            )

        def regroup(copy, w, c0, c1):
            if c0 == 0:
                wo_grouped[w] = grouped_pool.tile(
                    [P, N_TILE, PACK], BF16, name="grouped", tag="grouped", align_bytes=64
                )
            dst = wo_grouped[w][:, c0:c1, :].rearrange("p (c r) t -> p c t r", r=4)
            src = wo_raw[w][:, :, c0:c1].rearrange("p t (c r) -> p c t r", r=4)
            copy(out=dst, in_=src)

        def regroup_on_gpsimd(w):
            wo_grouped[w] = grouped_pool.tile(
                [P, N_TILE, PACK], BF16, name="grouped", tag="grouped", align_bytes=64
            )
            width = N_TILE // PIECES
            for c0 in range(0, N_TILE, width):
                nc.gpsimd.tensor_scalar(
                    out=wo_grouped[w][:, c0 : c0 + width, :].rearrange("p (c r) t -> p c t r", r=4),
                    in0=wo_raw[w][:, :, c0 : c0 + width].rearrange("p t (c r) -> p c t r", r=4),
                    scalar1=1.0, scalar2=0.0, op0=mybir.AluOpType.mult, op1=mybir.AluOpType.add,
                )

        def quantise_wo(w):
            nc.vector.quantize_mx(
                out=wo_codes[:, w, :].bitcast(FP8X4),
                scales=wo_scales[:, w, :],
                in_=wo_grouped[w][:].rearrange("p n t -> p (n t)"),
            )

        def new_sums(b):
            if b == 0:
                homes = [(psum_m, "m")] * ROW_TILES
            else:
                homes = [(psum_t, "t")] * 2 + [(psum_r, "r")] * 2
            return [pool.tile([P, N_TILE], F32, name="sums", tag=tag) for pool, tag in homes]

        def one_pass(b, j, bank, g, i, cols=slice(0, N_TILE)):
            u = b * PASSES + g
            w = j * PASSES + g
            rows = slice(i * P, (i + 1) * P)
            nc.tensor.matmul_mx(
                out=bank[:, cols],
                lhsT=ctx_codes[:, u, rows].bitcast(FP8X4),
                lhsT_scale=ctx_scales[:, u, rows],
                rhs=wo_codes[:, w, cols].bitcast(FP8X4),
                rhs_scale=wo_scales[:, w, cols],
                start=(g == 0),
                stop=(g == PASSES - 1),
            )

        def add_bias_and_store(b, j, sums, i0):
            cols = slice(j * N_TILE, (j + 1) * N_TILE)
            res = res_pool.tile([P, 2, N_TILE], F32, name="res", align_bytes=64)
            for i in (i0, i0 + 1):
                nc.vector.tensor_tensor(
                    out=res[:, i - i0, :], in0=sums[i][:], in1=bias_sb[:, cols],
                    op=mybir.AluOpType.add,
                )
            out_rows = out[b].rearrange("(p i) n -> p i n", i=ROW_TILES)
            nc.sync.dma_start(out=out_rows[:, i0 : i0 + 2, cols], in_=res[:])

        def finish(b, j):
            out_rows = out[b].rearrange("(p i) n -> p i n", i=ROW_TILES)
            whole = slice(0, N_TILE)
            halves = [slice(0, N_TILE // 2), slice(N_TILE // 2, N_TILE)]
            banks = new_sums(b)
            parts = [(i, whole, banks[i]) for i in range(ROW_TILES - 1)]
            spare = psum_m.tile([P, N_TILE], F32, name="sums", tag="m")
            parts += [(ROW_TILES - 1, halves[0], banks[ROW_TILES - 1]), (ROW_TILES - 1, halves[1], spare)]
            for i, cols, bank in parts:
                for g in range(PASSES):
                    one_pass(b, j, bank, g, i, cols)
                width = cols.stop - cols.start
                first = j * N_TILE + cols.start
                res = res_pool.tile([P, 2, N_TILE], F32, name="res", align_bytes=64)
                nc.vector.tensor_tensor(
                    out=res[:, 0, 0:width], in0=bank[:, cols], in1=bias_sb[:, first : first + width],
                    op=mybir.AluOpType.add,
                )
                nc.sync.dma_start(out=out_rows[:, i, first : first + width], in_=res[:, 0, 0:width])

        warm = psum_m.tile([P, P], F32, name="warm", tag="m")
        for n in range(WARM_UP):
            nc.tensor.matmul(warm[:], lhsT=ident[:], rhs=ident[:], start=True, stop=True)
        regroup_on_gpsimd(0)
        regroup_on_gpsimd(1)
        transpose_pair(0)
        nc.vector.reciprocal(out=rden[:], in_=den_bf[:])
        transpose_pair(1)
        for u in range(GROUPS):
            if u + 1 < GROUPS:
                transpose_pair(2 * u + 2)
            if u == 0:
                multiply_head(0)
                multiply_head(1)
            if u + 1 < GROUPS:
                transpose_pair(2 * u + 3)
            for n in range(PACK * u + (2 if u == 0 else 0), PACK * (u + 1)):
                multiply_head(n)
            if u == 6:
                quantise_wo(0)
            if u >= 1:
                turn_back(u - 1, 0)
                turn_back(u - 1, 1, on_scalar=True)
            if 2 <= u <= PASSES + 2:
                quantise_ctx(u - 2)
        for g in range(PASSES):
            load_wo_half(g)

        sums = [new_sums(0), None]
        regroup(nc.scalar.copy, 2, 0, N_TILE)
        quantise_wo(1)
        for i in range(ROW_TILES):
            one_pass(0, 0, sums[0][i], 0, i)
        turn_back(GROUPS - 1, 0)
        turn_back(GROUPS - 1, 1)
        sums[1] = new_sums(1)
        for i in range(ROW_TILES):
            one_pass(1, 0, sums[1][i], 0, i)
        for w in (3, 5, 6, 7):
            regroup(nc.scalar.copy, w, 0, N_TILE)
        quantise_ctx(PASSES + 1)
        quantise_wo(2)
        quantise_ctx(PASSES + 2)
        quantise_ctx(PASSES + 3)
        regroup(nc.vector.tensor_copy, 4, 0, N_TILE // 2)
        quantise_wo(3)
        regroup(nc.vector.tensor_copy, 4, N_TILE // 2, N_TILE)
        for g in range(1, PASSES):
            for b in range(B):
                for i in range(ROW_TILES):
                    one_pass(b, 0, sums[b][i], g, i)
        quantise_wo(5)
        quantise_wo(4)
        add_bias_and_store(0, 0, sums[0], 0)
        add_bias_and_store(0, 0, sums[0], 2)
        quantise_wo(6)
        add_bias_and_store(1, 0, sums[1], 0)
        quantise_wo(7)
        add_bias_and_store(1, 0, sums[1], 2)

        for j in range(1, N_CHUNKS):
            for b in range(B):
                if (j, b) == (N_CHUNKS - 1, B - 1):
                    finish(b, j)
                    continue
                sums = new_sums(b)
                for g in range(PASSES):
                    for i in range(ROW_TILES):
                        one_pass(b, j, sums[i], g, i)
                first = (j + 1) * PASSES
                more = j + 1 < N_CHUNKS
                if more and b == 0:
                    regroup(nc.vector.tensor_copy, first, 0, N_TILE // 2)
                    regroup(nc.scalar.copy, first, N_TILE // 2, N_TILE)
                    regroup(nc.scalar.copy, first + 1, 0, N_TILE)
                    add_bias_and_store(b, j, sums, 0)
                    quantise_wo(first)
                    add_bias_and_store(b, j, sums, 2)
                elif more:
                    regroup(nc.scalar.copy, first + 2, 0, N_TILE)
                    regroup(nc.scalar.copy, first + 3, 0, N_TILE)
                    quantise_wo(first + 1)
                    add_bias_and_store(b, j, sums, 0)
                    quantise_wo(first + 2)
                    add_bias_and_store(b, j, sums, 2)
                    quantise_wo(first + 3)
                else:
                    add_bias_and_store(b, j, sums, 0)
                    add_bias_and_store(b, j, sums, 2)
